import numpy as np
import ml_dtypes

BF16 = ml_dtypes.bfloat16


def bf(x):
    return np.asarray(x, np.float32).astype(BF16)


def f32(x):
    return np.asarray(x, np.float32)


def f64(x):
    return np.asarray(x).astype(np.float64)


def striped(idx):
    return np.tile(idx.reshape(-1, 16).T, (8, 1))


C, K, S, N = 256, 256, 512, 128
HALL_SCALE, CENT_SCALE, BIAS_SCALE = 3.0, 2.0, 0.5


def setup_inputs():
    return {"base": f32(np.random.standard_normal((C, S))), "x": bf(np.random.standard_normal((C, N))), "w_hall": bf(HALL_SCALE * np.random.standard_normal((C, K)) / np.sqrt(C)), "b_hall": f32(BIAS_SCALE * np.random.standard_normal((K, 1))), "centroids": bf(CENT_SCALE * np.random.standard_normal((K, C))), "b_sel": f32(BIAS_SCALE * np.random.standard_normal((C, 1))), "offs": striped(np.random.permutation(S)[:N])}


def reference(base, x, w_hall, b_hall, centroids, b_sel, offs):
    idx = offs[:16].T.reshape(-1)
    z = f64(w_hall).T @ f64(x) + f64(b_hall)
    e = np.exp(z - z.max(axis=0, keepdims=True))
    p = e / e.sum(axis=0, keepdims=True)
    mem = f64(centroids).T @ p
    sel = np.tanh(f64(x) + f64(b_sel))
    out = f64(base).copy()
    out[:, idx] = sel * mem
    return out

@@ -1,0 +1,75 @@
+import concourse.masks as masks
+import concourse.mybir as mybir
+
+P = 128
+C, K, S, N = 256, 256, 512, 128
+CB, KB = C // P, K // P
+FLOPS = 2 * C * K * N + 2 * K * C * N
+
+BF16, F32, U16 = mybir.dt.bfloat16, mybir.dt.float32, mybir.dt.uint16
+EXP, TANH = mybir.ActivationFunctionType.Exp, mybir.ActivationFunctionType.Tanh
+MULT = mybir.AluOpType.mult
+
+
+def tile_metaembedding_classifier_kernel(tc, base, x, w_hall, b_hall, centroids, b_sel, offs, out):
+    nc = tc.nc
+    with (
+        tc.tile_pool(name="held", bufs=1) as held,
+        tc.psum_pool(name="psum", bufs=1) as psum,
+    ):
+        x_sb = held.tile([P, CB, N], BF16, name="x_sb")
+        nc.sync.dma_start(x_sb[:], x.rearrange("(b p) j -> p b j", p=P))
+        w_sb = held.tile([P, CB, K], BF16, name="w_sb")
+        nc.scalar.dma_start(w_sb[:], w_hall.rearrange("(b p) k -> p b k", p=P))
+        b_hall_row = held.tile([1, K], F32, name="b_hall_row")
+        nc.sync.dma_start(b_hall_row[:], b_hall.rearrange("k o -> o k"))
+        offsets = held.tile([P, N // 16], U16, name="offsets")
+        nc.sync.dma_start(offsets[:], offs)
+        cent_sb = held.tile([P, KB, C], BF16, name="cent_sb")
+        nc.scalar.dma_start(cent_sb[:], centroids.rearrange("(b p) c -> p b c", p=P))
+        b_sel_sb = [held.tile([P, 1], F32, name=f"b_sel_sb{cb}") for cb in range(CB)]
+        window = [held.tile([P, S], F32, name=f"window{cb}") for cb in range(CB)]
+        for cb in range(CB):
+            nc.gpsimd.dma_start(b_sel_sb[cb][:], b_sel[cb * P : (cb + 1) * P, :])
+            nc.sync.dma_start(window[cb][:], base[cb * P : (cb + 1) * P, :])
+
+        identity = held.tile([P, P], BF16, name="identity")
+        masks.make_identity(nc, identity[:])
+        ones_row = held.tile([1, N], F32, name="ones_row")
+        nc.vector.memset(ones_row[:], 1.0)
+
+        z_t = psum.tile([P, K], F32, name="z_t")
+        nc.tensor.matmul(z_t[:], ones_row[:], b_hall_row[:], start=True, stop=False)
+        for b in range(CB):
+            nc.tensor.matmul(z_t[:], x_sb[:, b, :], w_sb[:, b, :], start=False, stop=(b == CB - 1))
+
+        neg_max = held.tile([P, 1], F32, name="neg_max")
+        nc.vector.reduce_max(neg_max[:], z_t[:], axis=mybir.AxisListType.X, negate=True)
+        e_t = held.tile([P, K], F32, name="e_t")
+        e_sum = held.tile([P, 1], F32, name="e_sum")
+        nc.scalar.activation(e_t[:], z_t[:], EXP, bias=neg_max[:], accum_out=e_sum[:])
+        r_sum = held.tile([P, 1], F32, name="r_sum")
+        nc.vector.reciprocal(r_sum[:], e_sum[:])
+        p_t = held.tile([P, K], BF16, name="p_t")
+        nc.vector.tensor_scalar_mul(p_t[:], e_t[:], r_sum[:])
+
+        sel = [held.tile([P, N], F32, name=f"sel{cb}") for cb in range(CB)]
+        for cb in range(CB):
+            nc.scalar.activation(sel[cb][:], x_sb[:, cb, :], TANH, bias=b_sel_sb[cb][:])
+
+        p_sb = [held.tile([P, N], BF16, name=f"p_sb{kb}") for kb in range(KB)]
+        for kb in range(KB):
+            p_ps = psum.tile([P, N], BF16, name=f"p_ps{kb}")
+            nc.tensor.transpose(p_ps[:], p_t[:, kb * P : (kb + 1) * P], identity[:])
+            nc.vector.tensor_copy(p_sb[kb][:], p_ps[:])
+
+        for cb in range(CB):
+            mem = psum.tile([P, N], F32, name=f"mem{cb}")
+            for kb in range(KB):
+                nc.tensor.matmul(
+                    mem[:], cent_sb[:, kb, cb * P : (cb + 1) * P], p_sb[kb][:], start=(kb == 0), stop=(kb == KB - 1)
+                )
+            mem_sb = held.tile([P, N], F32, name=f"mem_sb{cb}")
+            nc.scalar.copy(mem_sb[:], mem[:])
+            nc.vector.tensor_tensor(window[cb][:].indirect(offsets[:]), sel[cb][:], mem_sb[:], MULT)
+            nc.sync.dma_start(out[cb * P : (cb + 1) * P, :], window[cb][:])

@@ -21,55 +21,67 @@ def tile_metaembedding_classifier_kernel(tc, base, x, w_hall, b_hall, centroids,
         nc.sync.dma_start(x_sb[:], x.rearrange("(b p) j -> p b j", p=P))
         w_sb = held.tile([P, CB, K], BF16, name="w_sb")
         nc.scalar.dma_start(w_sb[:], w_hall.rearrange("(b p) k -> p b k", p=P))
-        b_hall_row = held.tile([1, K], F32, name="b_hall_row")
-        nc.sync.dma_start(b_hall_row[:], b_hall.rearrange("k o -> o k"))
+        b_hall_sb = held.tile([P, KB], F32, name="b_hall_sb")
+        b_sel_sb = held.tile([P, CB], F32, name="b_sel_sb")
+        with nc.allow_non_contiguous_dma(reason="one bias value to a partition"):
+            nc.sync.dma_start(b_hall_sb[:], b_hall.rearrange("(b p) o -> p (b o)", p=P))
+            nc.scalar.dma_start(b_sel_sb[:], b_sel.rearrange("(b p) o -> p (b o)", p=P))
         offsets = held.tile([P, N // 16], U16, name="offsets")
         nc.sync.dma_start(offsets[:], offs)
         cent_sb = held.tile([P, KB, C], BF16, name="cent_sb")
         nc.scalar.dma_start(cent_sb[:], centroids.rearrange("(b p) c -> p b c", p=P))
-        b_sel_sb = [held.tile([P, 1], F32, name=f"b_sel_sb{cb}") for cb in range(CB)]
         window = [held.tile([P, S], F32, name=f"window{cb}") for cb in range(CB)]
         for cb in range(CB):
-            nc.gpsimd.dma_start(b_sel_sb[cb][:], b_sel[cb * P : (cb + 1) * P, :])
             nc.sync.dma_start(window[cb][:], base[cb * P : (cb + 1) * P, :])
 
-        identity = held.tile([P, P], BF16, name="identity")
-        masks.make_identity(nc, identity[:])
-        ones_row = held.tile([1, N], F32, name="ones_row")
-        nc.vector.memset(ones_row[:], 1.0)
+        identity_bf = held.tile([P, P], BF16, name="identity_bf")
+        masks.make_identity(nc, identity_bf[:])
+        identity_f32 = held.tile([P, P], F32, name="identity_f32")
+        masks.make_identity(nc, identity_f32[:])
 
         z_t = psum.tile([P, K], F32, name="z_t")
-        nc.tensor.matmul(z_t[:], ones_row[:], b_hall_row[:], start=True, stop=False)
         for b in range(CB):
-            nc.tensor.matmul(z_t[:], x_sb[:, b, :], w_sb[:, b, :], start=False, stop=(b == CB - 1))
+            nc.tensor.matmul(z_t[:], x_sb[:, b, :], w_sb[:, b, :], start=(b == 0), stop=False)
+        for kb in range(KB):
+            nc.tensor.matmul(
+                z_t[:, kb * P : (kb + 1) * P],
+                b_hall_sb[:, kb : kb + 1].to_broadcast([P, P]),
+                identity_f32[:],
+                start=False,
+                stop=(kb == KB - 1),
+                is_transpose=True,
+            )
 
         neg_max = held.tile([P, 1], F32, name="neg_max")
         nc.vector.reduce_max(neg_max[:], z_t[:], axis=mybir.AxisListType.X, negate=True)
-        e_t = held.tile([P, K], F32, name="e_t")
+        e_t = held.tile([P, K], BF16, name="e_t")
         e_sum = held.tile([P, 1], F32, name="e_sum")
         nc.scalar.activation(e_t[:], z_t[:], EXP, bias=neg_max[:], accum_out=e_sum[:])
+
+        e_sb = [held.tile([P, N], BF16, name=f"e_sb{kb}") for kb in range(KB)]
+        for kb in range(KB):
+            e_ps = psum.tile([P, N], BF16, name=f"e_ps{kb}")
+            nc.tensor.transpose(e_ps[:], e_t[:, kb * P : (kb + 1) * P], identity_bf[:])
+            nc.vector.tensor_copy(e_sb[kb][:], e_ps[:])
+
         r_sum = held.tile([P, 1], F32, name="r_sum")
         nc.vector.reciprocal(r_sum[:], e_sum[:])
-        p_t = held.tile([P, K], BF16, name="p_t")
-        nc.vector.tensor_scalar_mul(p_t[:], e_t[:], r_sum[:])
+        r_all = psum.tile([P, N], F32, name="r_all")
+        nc.tensor.transpose(r_all[:], r_sum[:, 0:1].to_broadcast([P, P]), identity_f32[:])
 
         sel = [held.tile([P, N], F32, name=f"sel{cb}") for cb in range(CB)]
+        sel_r = [held.tile([P, N], F32, name=f"sel_r{cb}") for cb in range(CB)]
         for cb in range(CB):
-            nc.scalar.activation(sel[cb][:], x_sb[:, cb, :], TANH, bias=b_sel_sb[cb][:])
-
-        p_sb = [held.tile([P, N], BF16, name=f"p_sb{kb}") for kb in range(KB)]
-        for kb in range(KB):
-            p_ps = psum.tile([P, N], BF16, name=f"p_ps{kb}")
-            nc.tensor.transpose(p_ps[:], p_t[:, kb * P : (kb + 1) * P], identity[:])
-            nc.vector.tensor_copy(p_sb[kb][:], p_ps[:])
+            nc.scalar.activation(sel[cb][:], x_sb[:, cb, :], TANH, bias=b_sel_sb[:, cb : cb + 1])
+            nc.vector.tensor_tensor(sel_r[cb][:], sel[cb][:], r_all[:], MULT)
 
         for cb in range(CB):
             mem = psum.tile([P, N], F32, name=f"mem{cb}")
             for kb in range(KB):
                 nc.tensor.matmul(
-                    mem[:], cent_sb[:, kb, cb * P : (cb + 1) * P], p_sb[kb][:], start=(kb == 0), stop=(kb == KB - 1)
+                    mem[:], cent_sb[:, kb, cb * P : (cb + 1) * P], e_sb[kb][:], start=(kb == 0), stop=(kb == KB - 1)
                 )
             mem_sb = held.tile([P, N], F32, name=f"mem_sb{cb}")
             nc.scalar.copy(mem_sb[:], mem[:])
-            nc.vector.tensor_tensor(window[cb][:].indirect(offsets[:]), sel[cb][:], mem_sb[:], MULT)
+            nc.vector.tensor_tensor(window[cb][:].indirect(offsets[:]), sel_r[cb][:], mem_sb[:], MULT)
             nc.sync.dma_start(out[cb * P : (cb + 1) * P, :], window[cb][:])

@@ -34,23 +34,21 @@ def tile_metaembedding_classifier_kernel(tc, base, x, w_hall, b_hall, centroids,
         for cb in range(CB):
             nc.sync.dma_start(window[cb][:], base[cb * P : (cb + 1) * P, :])
 
-        identity_bf = held.tile([P, P], BF16, name="identity_bf")
-        masks.make_identity(nc, identity_bf[:])
-        identity_f32 = held.tile([P, P], F32, name="identity_f32")
-        masks.make_identity(nc, identity_f32[:])
+        identity = held.tile([P, P], F32, name="identity")
+        masks.make_identity(nc, identity[:])
+
+        def add_along_free(acc, column, start, stop):
+            nc.tensor.matmul(acc, column.to_broadcast([P, P]), identity[:], start=start, stop=stop, is_transpose=True)
 
         z_t = psum.tile([P, K], F32, name="z_t")
         for b in range(CB):
             nc.tensor.matmul(z_t[:], x_sb[:, b, :], w_sb[:, b, :], start=(b == 0), stop=False)
         for kb in range(KB):
-            nc.tensor.matmul(
-                z_t[:, kb * P : (kb + 1) * P],
-                b_hall_sb[:, kb : kb + 1].to_broadcast([P, P]),
-                identity_f32[:],
-                start=False,
-                stop=(kb == KB - 1),
-                is_transpose=True,
-            )
+            add_along_free(z_t[:, kb * P : (kb + 1) * P], b_hall_sb[:, kb : kb + 1], start=False, stop=(kb == KB - 1))
+
+        sel = [held.tile([P, N], F32, name=f"sel{cb}") for cb in range(CB)]
+        for cb in range(CB):
+            nc.scalar.activation(sel[cb][:], x_sb[:, cb, :], TANH, bias=b_sel_sb[:, cb : cb + 1])
 
         neg_max = held.tile([P, 1], F32, name="neg_max")
         nc.vector.reduce_max(neg_max[:], z_t[:], axis=mybir.AxisListType.X, negate=True)
@@ -60,19 +58,18 @@ def tile_metaembedding_classifier_kernel(tc, base, x, w_hall, b_hall, centroids,
 
         e_sb = [held.tile([P, N], BF16, name=f"e_sb{kb}") for kb in range(KB)]
         for kb in range(KB):
-            e_ps = psum.tile([P, N], BF16, name=f"e_ps{kb}")
-            nc.tensor.transpose(e_ps[:], e_t[:, kb * P : (kb + 1) * P], identity_bf[:])
-            nc.vector.tensor_copy(e_sb[kb][:], e_ps[:])
+            z = psum.tile([P, N], F32, name=f"z{kb}")
+            add_along_free(z[:], neg_max[:, 0:1], start=True, stop=False)
+            for b in range(CB):
+                nc.tensor.matmul(z[:], w_sb[:, b, kb * P : (kb + 1) * P], x_sb[:, b, :], start=False, stop=(b == CB - 1))
+            nc.scalar.activation(e_sb[kb][:], z[:], EXP, bias=b_hall_sb[:, kb : kb + 1])
 
         r_sum = held.tile([P, 1], F32, name="r_sum")
         nc.vector.reciprocal(r_sum[:], e_sum[:])
         r_all = psum.tile([P, N], F32, name="r_all")
-        nc.tensor.transpose(r_all[:], r_sum[:, 0:1].to_broadcast([P, P]), identity_f32[:])
-
-        sel = [held.tile([P, N], F32, name=f"sel{cb}") for cb in range(CB)]
+        nc.tensor.transpose(r_all[:], r_sum[:, 0:1].to_broadcast([P, P]), identity[:])
         sel_r = [held.tile([P, N], F32, name=f"sel_r{cb}") for cb in range(CB)]
         for cb in range(CB):
-            nc.scalar.activation(sel[cb][:], x_sb[:, cb, :], TANH, bias=b_sel_sb[:, cb : cb + 1])
             nc.vector.tensor_tensor(sel_r[cb][:], sel[cb][:], r_all[:], MULT)
 
         for cb in range(CB):

@@ -46,9 +46,9 @@ def tile_metaembedding_classifier_kernel(tc, base, x, w_hall, b_hall, centroids,
         for kb in range(KB):
             add_along_free(z_t[:, kb * P : (kb + 1) * P], b_hall_sb[:, kb : kb + 1], start=False, stop=(kb == KB - 1))
 
-        sel = [held.tile([P, N], F32, name=f"sel{cb}") for cb in range(CB)]
+        sel = held.tile([P, CB, N], F32, name="sel")
         for cb in range(CB):
-            nc.scalar.activation(sel[cb][:], x_sb[:, cb, :], TANH, bias=b_sel_sb[:, cb : cb + 1])
+            nc.scalar.activation(sel[:, cb, :], x_sb[:, cb, :], TANH, bias=b_sel_sb[:, cb : cb + 1])
 
         neg_max = held.tile([P, 1], F32, name="neg_max")
         nc.vector.reduce_max(neg_max[:], z_t[:], axis=mybir.AxisListType.X, negate=True)
@@ -68,9 +68,8 @@ def tile_metaembedding_classifier_kernel(tc, base, x, w_hall, b_hall, centroids,
         nc.vector.reciprocal(r_sum[:], e_sum[:])
         r_all = psum.tile([P, N], F32, name="r_all")
         nc.tensor.transpose(r_all[:], r_sum[:, 0:1].to_broadcast([P, P]), identity[:])
-        sel_r = [held.tile([P, N], F32, name=f"sel_r{cb}") for cb in range(CB)]
-        for cb in range(CB):
-            nc.vector.tensor_tensor(sel_r[cb][:], sel[cb][:], r_all[:], MULT)
+        sel_r = held.tile([P, CB, N], F32, name="sel_r")
+        nc.vector.tensor_tensor(sel_r[:], sel[:], r_all[:].unsqueeze(1).to_broadcast([P, CB, N]), MULT)
 
         for cb in range(CB):
             mem = psum.tile([P, N], F32, name=f"mem{cb}")
@@ -79,6 +78,11 @@ def tile_metaembedding_classifier_kernel(tc, base, x, w_hall, b_hall, centroids,
                     mem[:], cent_sb[:, kb, cb * P : (cb + 1) * P], e_sb[kb][:], start=(kb == 0), stop=(kb == KB - 1)
                 )
             mem_sb = held.tile([P, N], F32, name=f"mem_sb{cb}")
-            nc.scalar.copy(mem_sb[:], mem[:])
-            nc.vector.tensor_tensor(window[cb][:].indirect(offsets[:]), sel_r[cb][:], mem_sb[:], MULT)
-            nc.sync.dma_start(out[cb * P : (cb + 1) * P, :], window[cb][:])
+            if cb == 0:
+                nc.vector.tensor_copy(mem_sb[:], mem[:])
+            else:
+                nc.scalar.copy(mem_sb[:], mem[:])
+            nc.vector.tensor_tensor(window[cb][:].indirect(offsets[:]), sel_r[:, cb, :], mem_sb[:], MULT)
+            rows = slice(cb * P, (cb + 1) * P)
+            nc.sync.dma_start(out[rows, 0 : S // 2], window[cb][:, 0 : S // 2])
+            nc.scalar.dma_start(out[rows, S // 2 : S], window[cb][:, S // 2 : S])

@@ -9,6 +9,7 @@ FLOPS = 2 * C * K * N + 2 * K * C * N
 BF16, F32, U16 = mybir.dt.bfloat16, mybir.dt.float32, mybir.dt.uint16
 EXP, TANH = mybir.ActivationFunctionType.Exp, mybir.ActivationFunctionType.Tanh
 MULT = mybir.AluOpType.mult
+WARM_UP = 6
 
 
 def tile_metaembedding_classifier_kernel(tc, base, x, w_hall, b_hall, centroids, b_sel, offs, out):
@@ -34,6 +35,12 @@ def tile_metaembedding_classifier_kernel(tc, base, x, w_hall, b_hall, centroids,
         for cb in range(CB):
             nc.sync.dma_start(window[cb][:], base[cb * P : (cb + 1) * P, :])
 
+        zeros = held.tile([P, S], BF16, name="zeros")
+        nc.gpsimd.memset(zeros[:], 0.0)
+        unused = psum.tile([P, S], F32, name="unused")
+        for i in range(WARM_UP):
+            nc.tensor.matmul(unused[:], zeros[:, 0:P], zeros[:], start=True, stop=True)
+
         identity = held.tile([P, P], F32, name="identity")
         masks.make_identity(nc, identity[:])
 
@@ -46,9 +53,9 @@ def tile_metaembedding_classifier_kernel(tc, base, x, w_hall, b_hall, centroids,
         for kb in range(KB):
             add_along_free(z_t[:, kb * P : (kb + 1) * P], b_hall_sb[:, kb : kb + 1], start=False, stop=(kb == KB - 1))
 
-        sel = held.tile([P, CB, N], F32, name="sel")
+        sel = [held.tile([P, N], F32, name=f"sel{cb}") for cb in range(CB)]
         for cb in range(CB):
-            nc.scalar.activation(sel[:, cb, :], x_sb[:, cb, :], TANH, bias=b_sel_sb[:, cb : cb + 1])
+            nc.scalar.activation(sel[cb][:], x_sb[:, cb, :], TANH, bias=b_sel_sb[:, cb : cb + 1])
 
         neg_max = held.tile([P, 1], F32, name="neg_max")
         nc.vector.reduce_max(neg_max[:], z_t[:], axis=mybir.AxisListType.X, negate=True)
@@ -68,8 +75,9 @@ def tile_metaembedding_classifier_kernel(tc, base, x, w_hall, b_hall, centroids,
         nc.vector.reciprocal(r_sum[:], e_sum[:])
         r_all = psum.tile([P, N], F32, name="r_all")
         nc.tensor.transpose(r_all[:], r_sum[:, 0:1].to_broadcast([P, P]), identity[:])
-        sel_r = held.tile([P, CB, N], F32, name="sel_r")
-        nc.vector.tensor_tensor(sel_r[:], sel[:], r_all[:].unsqueeze(1).to_broadcast([P, CB, N]), MULT)
+        sel_r = [held.tile([P, N], F32, name=f"sel_r{cb}") for cb in range(CB)]
+        for cb in range(CB):
+            nc.vector.tensor_tensor(sel_r[cb][:], sel[cb][:], r_all[:], MULT)
 
         for cb in range(CB):
             mem = psum.tile([P, N], F32, name=f"mem{cb}")
@@ -78,11 +86,6 @@ def tile_metaembedding_classifier_kernel(tc, base, x, w_hall, b_hall, centroids,
                     mem[:], cent_sb[:, kb, cb * P : (cb + 1) * P], e_sb[kb][:], start=(kb == 0), stop=(kb == KB - 1)
                 )
             mem_sb = held.tile([P, N], F32, name=f"mem_sb{cb}")
-            if cb == 0:
-                nc.vector.tensor_copy(mem_sb[:], mem[:])
-            else:
-                nc.scalar.copy(mem_sb[:], mem[:])
-            nc.vector.tensor_tensor(window[cb][:].indirect(offsets[:]), sel_r[:, cb, :], mem_sb[:], MULT)
-            rows = slice(cb * P, (cb + 1) * P)
-            nc.sync.dma_start(out[rows, 0 : S // 2], window[cb][:, 0 : S // 2])
-            nc.scalar.dma_start(out[rows, S // 2 : S], window[cb][:, S // 2 : S])
+            nc.scalar.copy(mem_sb[:], mem[:])
+            nc.vector.tensor_tensor(window[cb][:].indirect(offsets[:]), sel_r[cb][:], mem_sb[:], MULT)
+            nc.sync.dma_start(out[cb * P : (cb + 1) * P, :], window[cb][:])

@@ -9,7 +9,7 @@ FLOPS = 2 * C * K * N + 2 * K * C * N
 BF16, F32, U16 = mybir.dt.bfloat16, mybir.dt.float32, mybir.dt.uint16
 EXP, TANH = mybir.ActivationFunctionType.Exp, mybir.ActivationFunctionType.Tanh
 MULT = mybir.AluOpType.mult
-WARM_UP = 6
+WARM_UP = 4
 
 
 def tile_metaembedding_classifier_kernel(tc, base, x, w_hall, b_hall, centroids, b_sel, offs, out):
@@ -35,11 +35,11 @@ def tile_metaembedding_classifier_kernel(tc, base, x, w_hall, b_hall, centroids,
         for cb in range(CB):
             nc.sync.dma_start(window[cb][:], base[cb * P : (cb + 1) * P, :])
 
-        zeros = held.tile([P, S], BF16, name="zeros")
+        zeros = held.tile([P, P], BF16, name="zeros")
         nc.gpsimd.memset(zeros[:], 0.0)
-        unused = psum.tile([P, S], F32, name="unused")
+        unused = psum.tile([P, 4, P], F32, name="unused")
         for i in range(WARM_UP):
-            nc.tensor.matmul(unused[:], zeros[:, 0:P], zeros[:], start=True, stop=True)
+            nc.tensor.matmul(unused[:], zeros[:], zeros[:].unsqueeze(1).to_broadcast([P, 4, P]), start=True, stop=True)
 
         identity = held.tile([P, P], F32, name="identity")
         masks.make_identity(nc, identity[:])

@@ -1,4 +1,3 @@
-import concourse.masks as masks
 import concourse.mybir as mybir
 
 P = 128
@@ -40,44 +39,28 @@ def tile_metaembedding_classifier_kernel(tc, base, x, w_hall, b_hall, centroids,
         unused = psum.tile([P, 4, P], F32, name="unused")
         for i in range(WARM_UP):
             nc.tensor.matmul(unused[:], zeros[:], zeros[:].unsqueeze(1).to_broadcast([P, 4, P]), start=True, stop=True)
-
-        identity = held.tile([P, P], F32, name="identity")
-        masks.make_identity(nc, identity[:])
-
-        def add_along_free(acc, column, start, stop):
-            nc.tensor.matmul(acc, column.to_broadcast([P, P]), identity[:], start=start, stop=stop, is_transpose=True)
-
-        z_t = psum.tile([P, K], F32, name="z_t")
-        for b in range(CB):
-            nc.tensor.matmul(z_t[:], x_sb[:, b, :], w_sb[:, b, :], start=(b == 0), stop=False)
-        for kb in range(KB):
-            add_along_free(z_t[:, kb * P : (kb + 1) * P], b_hall_sb[:, kb : kb + 1], start=False, stop=(kb == KB - 1))
+        ones = held.tile([P, P], BF16, name="ones")
+        nc.gpsimd.memset(ones[:], 1.0)
 
         sel = [held.tile([P, N], F32, name=f"sel{cb}") for cb in range(CB)]
         for cb in range(CB):
             nc.scalar.activation(sel[cb][:], x_sb[:, cb, :], TANH, bias=b_sel_sb[:, cb : cb + 1])
 
-        neg_max = held.tile([P, 1], F32, name="neg_max")
-        nc.vector.reduce_max(neg_max[:], z_t[:], axis=mybir.AxisListType.X, negate=True)
-        e_t = held.tile([P, K], BF16, name="e_t")
-        e_sum = held.tile([P, 1], F32, name="e_sum")
-        nc.scalar.activation(e_t[:], z_t[:], EXP, bias=neg_max[:], accum_out=e_sum[:])
-
         e_sb = [held.tile([P, N], BF16, name=f"e_sb{kb}") for kb in range(KB)]
         for kb in range(KB):
             z = psum.tile([P, N], F32, name=f"z{kb}")
-            add_along_free(z[:], neg_max[:, 0:1], start=True, stop=False)
             for b in range(CB):
-                nc.tensor.matmul(z[:], w_sb[:, b, kb * P : (kb + 1) * P], x_sb[:, b, :], start=False, stop=(b == CB - 1))
+                nc.tensor.matmul(z[:], w_sb[:, b, kb * P : (kb + 1) * P], x_sb[:, b, :], start=(b == 0), stop=(b == CB - 1))
             nc.scalar.activation(e_sb[kb][:], z[:], EXP, bias=b_hall_sb[:, kb : kb + 1])
 
-        r_sum = held.tile([P, 1], F32, name="r_sum")
+        e_sum = psum.tile([P, N], F32, name="e_sum")
+        for kb in range(KB):
+            nc.tensor.matmul(e_sum[:], ones[:], e_sb[kb][:], start=(kb == 0), stop=(kb == KB - 1))
+        r_sum = held.tile([P, N], F32, name="r_sum")
         nc.vector.reciprocal(r_sum[:], e_sum[:])
-        r_all = psum.tile([P, N], F32, name="r_all")
-        nc.tensor.transpose(r_all[:], r_sum[:, 0:1].to_broadcast([P, P]), identity[:])
         sel_r = [held.tile([P, N], F32, name=f"sel_r{cb}") for cb in range(CB)]
         for cb in range(CB):
-            nc.vector.tensor_tensor(sel_r[cb][:], sel[cb][:], r_all[:], MULT)
+            nc.vector.tensor_tensor(sel_r[cb][:], sel[cb][:], r_sum[:], MULT)
 
         for cb in range(CB):
             mem = psum.tile([P, N], F32, name=f"mem{cb}")

@@ -1,3 +1,4 @@
+import concourse.masks as masks
 import concourse.mybir as mybir
 
 P = 128
@@ -20,16 +21,16 @@ def tile_metaembedding_classifier_kernel(tc, base, x, w_hall, b_hall, centroids,
         x_sb = held.tile([P, CB, N], BF16, name="x_sb")
         nc.sync.dma_start(x_sb[:], x.rearrange("(b p) j -> p b j", p=P))
         w_sb = held.tile([P, CB, K], BF16, name="w_sb")
-        nc.scalar.dma_start(w_sb[:], w_hall.rearrange("(b p) k -> p b k", p=P))
+        nc.sync.dma_start(w_sb[:], w_hall.rearrange("(b p) k -> p b k", p=P))
         b_hall_sb = held.tile([P, KB], F32, name="b_hall_sb")
         b_sel_sb = held.tile([P, CB], F32, name="b_sel_sb")
         with nc.allow_non_contiguous_dma(reason="one bias value to a partition"):
             nc.sync.dma_start(b_hall_sb[:], b_hall.rearrange("(b p) o -> p (b o)", p=P))
-            nc.scalar.dma_start(b_sel_sb[:], b_sel.rearrange("(b p) o -> p (b o)", p=P))
+            nc.sync.dma_start(b_sel_sb[:], b_sel.rearrange("(b p) o -> p (b o)", p=P))
+        cent_sb = held.tile([P, KB, C], BF16, name="cent_sb")
+        nc.sync.dma_start(cent_sb[:], centroids.rearrange("(b p) c -> p b c", p=P))
         offsets = held.tile([P, N // 16], U16, name="offsets")
         nc.sync.dma_start(offsets[:], offs)
-        cent_sb = held.tile([P, KB, C], BF16, name="cent_sb")
-        nc.scalar.dma_start(cent_sb[:], centroids.rearrange("(b p) c -> p b c", p=P))
         window = [held.tile([P, S], F32, name=f"window{cb}") for cb in range(CB)]
         for cb in range(CB):
             nc.sync.dma_start(window[cb][:], base[cb * P : (cb + 1) * P, :])
@@ -39,8 +40,13 @@ def tile_metaembedding_classifier_kernel(tc, base, x, w_hall, b_hall, centroids,
         unused = psum.tile([P, 4, P], F32, name="unused")
         for i in range(WARM_UP):
             nc.tensor.matmul(unused[:], zeros[:], zeros[:].unsqueeze(1).to_broadcast([P, 4, P]), start=True, stop=True)
-        ones = held.tile([P, P], BF16, name="ones")
+        ones = held.tile([P, 1], BF16, name="ones")
         nc.gpsimd.memset(ones[:], 1.0)
+        identity = held.tile([P, P], F32, name="identity")
+        masks.make_identity(nc, identity[:])
+
+        early = held.tile([P, 1], F32, name="early")
+        nc.scalar.activation(early[:], zeros[:, 0:1], EXP)
 
         sel = [held.tile([P, N], F32, name=f"sel{cb}") for cb in range(CB)]
         for cb in range(CB):
@@ -53,14 +59,17 @@ def tile_metaembedding_classifier_kernel(tc, base, x, w_hall, b_hall, centroids,
                 nc.tensor.matmul(z[:], w_sb[:, b, kb * P : (kb + 1) * P], x_sb[:, b, :], start=(b == 0), stop=(b == CB - 1))
             nc.scalar.activation(e_sb[kb][:], z[:], EXP, bias=b_hall_sb[:, kb : kb + 1])
 
-        e_sum = psum.tile([P, N], F32, name="e_sum")
+        e_sum = psum.tile([P, 1], F32, name="e_sum")
         for kb in range(KB):
-            nc.tensor.matmul(e_sum[:], ones[:], e_sb[kb][:], start=(kb == 0), stop=(kb == KB - 1))
-        r_sum = held.tile([P, N], F32, name="r_sum")
+            nc.tensor.matmul(e_sum[:], e_sb[kb][:], ones[:, 0:1], start=(kb == 0), stop=(kb == KB - 1))
+        r_sum = held.tile([P, 1], F32, name="r_sum")
         nc.vector.reciprocal(r_sum[:], e_sum[:])
+
+        r_all = psum.tile([P, N], F32, name="r_all")
+        nc.tensor.transpose(r_all[:], r_sum[:, 0:1].to_broadcast([P, P]), identity[:])
         sel_r = [held.tile([P, N], F32, name=f"sel_r{cb}") for cb in range(CB)]
         for cb in range(CB):
-            nc.vector.tensor_tensor(sel_r[cb][:], sel[cb][:], r_sum[:], MULT)
+            nc.vector.tensor_tensor(sel_r[cb][:], sel[cb][:], r_all[:], MULT)
 
         for cb in range(CB):
             mem = psum.tile([P, N], F32, name=f"mem{cb}")

@@ -9,7 +9,7 @@ FLOPS = 2 * C * K * N + 2 * K * C * N
 BF16, F32, U16 = mybir.dt.bfloat16, mybir.dt.float32, mybir.dt.uint16
 EXP, TANH = mybir.ActivationFunctionType.Exp, mybir.ActivationFunctionType.Tanh
 MULT = mybir.AluOpType.mult
-WARM_UP = 4
+WARM_UP = 3
 
 
 def tile_metaembedding_classifier_kernel(tc, base, x, w_hall, b_hall, centroids, b_sel, offs, out):
@@ -19,21 +19,20 @@ def tile_metaembedding_classifier_kernel(tc, base, x, w_hall, b_hall, centroids,
         tc.psum_pool(name="psum", bufs=1) as psum,
     ):
         x_sb = held.tile([P, CB, N], BF16, name="x_sb")
-        nc.sync.dma_start(x_sb[:], x.rearrange("(b p) j -> p b j", p=P))
+        nc.sync.dma_start(x_sb[:], x.rearrange("(p b) j -> p b j", b=CB))
         w_sb = held.tile([P, CB, K], BF16, name="w_sb")
-        nc.sync.dma_start(w_sb[:], w_hall.rearrange("(b p) k -> p b k", p=P))
+        nc.sync.dma_start(w_sb[:], w_hall.rearrange("(p b) k -> p b k", b=CB))
         b_hall_sb = held.tile([P, KB], F32, name="b_hall_sb")
-        b_sel_sb = held.tile([P, CB], F32, name="b_sel_sb")
-        with nc.allow_non_contiguous_dma(reason="one bias value to a partition"):
-            nc.sync.dma_start(b_hall_sb[:], b_hall.rearrange("(b p) o -> p (b o)", p=P))
-            nc.sync.dma_start(b_sel_sb[:], b_sel.rearrange("(b p) o -> p (b o)", p=P))
+        nc.sync.dma_start(b_hall_sb[:], b_hall.rearrange("(p b) o -> p (b o)", b=KB))
         cent_sb = held.tile([P, KB, C], BF16, name="cent_sb")
-        nc.sync.dma_start(cent_sb[:], centroids.rearrange("(b p) c -> p b c", p=P))
+        nc.sync.dma_start(cent_sb[:], centroids.rearrange("(p b) c -> p b c", b=KB))
+        b_sel_sb = held.tile([P, CB], F32, name="b_sel_sb")
+        nc.sync.dma_start(b_sel_sb[:], b_sel.rearrange("(p b) o -> p (b o)", b=CB))
         offsets = held.tile([P, N // 16], U16, name="offsets")
         nc.sync.dma_start(offsets[:], offs)
         window = [held.tile([P, S], F32, name=f"window{cb}") for cb in range(CB)]
         for cb in range(CB):
-            nc.sync.dma_start(window[cb][:], base[cb * P : (cb + 1) * P, :])
+            nc.sync.dma_start(window[cb][:], base.rearrange("(p b) s -> p b s", b=CB)[:, cb, :])
 
         zeros = held.tile([P, P], BF16, name="zeros")
         nc.gpsimd.memset(zeros[:], 0.0)
@@ -48,16 +47,16 @@ def tile_metaembedding_classifier_kernel(tc, base, x, w_hall, b_hall, centroids,
         early = held.tile([P, 1], F32, name="early")
         nc.scalar.activation(early[:], zeros[:, 0:1], EXP)
 
-        sel = [held.tile([P, N], F32, name=f"sel{cb}") for cb in range(CB)]
-        for cb in range(CB):
-            nc.scalar.activation(sel[cb][:], x_sb[:, cb, :], TANH, bias=b_sel_sb[:, cb : cb + 1])
-
         e_sb = [held.tile([P, N], BF16, name=f"e_sb{kb}") for kb in range(KB)]
         for kb in range(KB):
             z = psum.tile([P, N], F32, name=f"z{kb}")
             for b in range(CB):
-                nc.tensor.matmul(z[:], w_sb[:, b, kb * P : (kb + 1) * P], x_sb[:, b, :], start=(b == 0), stop=(b == CB - 1))
+                nc.tensor.matmul(z[:], w_sb[:, b, kb::KB], x_sb[:, b, :], start=(b == 0), stop=(b == CB - 1))
             nc.scalar.activation(e_sb[kb][:], z[:], EXP, bias=b_hall_sb[:, kb : kb + 1])
+
+        sel = [held.tile([P, N], F32, name=f"sel{cb}") for cb in range(CB)]
+        for cb in range(CB):
+            nc.scalar.activation(sel[cb][:], x_sb[:, cb, :], TANH, bias=b_sel_sb[:, cb : cb + 1])
 
         e_sum = psum.tile([P, 1], F32, name="e_sum")
         for kb in range(KB):
@@ -74,10 +73,8 @@ def tile_metaembedding_classifier_kernel(tc, base, x, w_hall, b_hall, centroids,
         for cb in range(CB):
             mem = psum.tile([P, N], F32, name=f"mem{cb}")
             for kb in range(KB):
-                nc.tensor.matmul(
-                    mem[:], cent_sb[:, kb, cb * P : (cb + 1) * P], e_sb[kb][:], start=(kb == 0), stop=(kb == KB - 1)
-                )
+                nc.tensor.matmul(mem[:], cent_sb[:, kb, cb::CB], e_sb[kb][:], start=(kb == 0), stop=(kb == KB - 1))
             mem_sb = held.tile([P, N], F32, name=f"mem_sb{cb}")
             nc.scalar.copy(mem_sb[:], mem[:])
             nc.vector.tensor_tensor(window[cb][:].indirect(offsets[:]), sel_r[cb][:], mem_sb[:], MULT)
-            nc.sync.dma_start(out[cb * P : (cb + 1) * P, :], window[cb][:])
+            nc.sync.dma_start(out.rearrange("(p b) s -> p b s", b=CB)[:, cb, :], window[cb][:])

@@ -22,12 +22,12 @@ def tile_metaembedding_classifier_kernel(tc, base, x, w_hall, b_hall, centroids,
         nc.sync.dma_start(x_sb[:], x.rearrange("(p b) j -> p b j", b=CB))
         w_sb = held.tile([P, CB, K], BF16, name="w_sb")
         nc.sync.dma_start(w_sb[:], w_hall.rearrange("(p b) k -> p b k", b=CB))
+        b_sel_sb = held.tile([P, CB], F32, name="b_sel_sb")
+        nc.sync.dma_start(b_sel_sb[:], b_sel.rearrange("(p b) o -> p (b o)", b=CB))
         b_hall_sb = held.tile([P, KB], F32, name="b_hall_sb")
         nc.sync.dma_start(b_hall_sb[:], b_hall.rearrange("(p b) o -> p (b o)", b=KB))
         cent_sb = held.tile([P, KB, C], BF16, name="cent_sb")
         nc.sync.dma_start(cent_sb[:], centroids.rearrange("(p b) c -> p b c", b=KB))
-        b_sel_sb = held.tile([P, CB], F32, name="b_sel_sb")
-        nc.sync.dma_start(b_sel_sb[:], b_sel.rearrange("(p b) o -> p (b o)", b=CB))
         offsets = held.tile([P, N // 16], U16, name="offsets")
         nc.sync.dma_start(offsets[:], offs)
         window = [held.tile([P, S], F32, name=f"window{cb}") for cb in range(CB)]
@@ -47,16 +47,16 @@ def tile_metaembedding_classifier_kernel(tc, base, x, w_hall, b_hall, centroids,
         early = held.tile([P, 1], F32, name="early")
         nc.scalar.activation(early[:], zeros[:, 0:1], EXP)
 
+        sel = [held.tile([P, N], F32, name=f"sel{cb}") for cb in range(CB)]
+        for cb in range(CB):
+            nc.scalar.activation(sel[cb][:], x_sb[:, cb, :], TANH, bias=b_sel_sb[:, cb : cb + 1])
+
         e_sb = [held.tile([P, N], BF16, name=f"e_sb{kb}") for kb in range(KB)]
         for kb in range(KB):
             z = psum.tile([P, N], F32, name=f"z{kb}")
             for b in range(CB):
                 nc.tensor.matmul(z[:], w_sb[:, b, kb::KB], x_sb[:, b, :], start=(b == 0), stop=(b == CB - 1))
             nc.scalar.activation(e_sb[kb][:], z[:], EXP, bias=b_hall_sb[:, kb : kb + 1])
-
-        sel = [held.tile([P, N], F32, name=f"sel{cb}") for cb in range(CB)]
-        for cb in range(CB):
-            nc.scalar.activation(sel[cb][:], x_sb[:, cb, :], TANH, bias=b_sel_sb[:, cb : cb + 1])
 
         e_sum = psum.tile([P, 1], F32, name="e_sum")
         for kb in range(KB):
@@ -66,15 +66,17 @@ def tile_metaembedding_classifier_kernel(tc, base, x, w_hall, b_hall, centroids,
 
         r_all = psum.tile([P, N], F32, name="r_all")
         nc.tensor.transpose(r_all[:], r_sum[:, 0:1].to_broadcast([P, P]), identity[:])
-        sel_r = [held.tile([P, N], F32, name=f"sel_r{cb}") for cb in range(CB)]
-        for cb in range(CB):
-            nc.vector.tensor_tensor(sel_r[cb][:], sel[cb][:], r_all[:], MULT)
 
+        mem_sb = [held.tile([P, N], F32, name=f"mem_sb{cb}") for cb in range(CB)]
         for cb in range(CB):
             mem = psum.tile([P, N], F32, name=f"mem{cb}")
             for kb in range(KB):
                 nc.tensor.matmul(mem[:], cent_sb[:, kb, cb::CB], e_sb[kb][:], start=(kb == 0), stop=(kb == KB - 1))
-            mem_sb = held.tile([P, N], F32, name=f"mem_sb{cb}")
-            nc.scalar.copy(mem_sb[:], mem[:])
-            nc.vector.tensor_tensor(window[cb][:].indirect(offsets[:]), sel_r[cb][:], mem_sb[:], MULT)
+            nc.vector.tensor_copy(mem_sb[cb][:], mem[:])
+
+        sel_r = [held.tile([P, N], F32, name=f"sel_r{cb}") for cb in range(CB)]
+        for cb in range(CB):
+            nc.vector.tensor_tensor(sel_r[cb][:], sel[cb][:], r_all[:], MULT)
+        for cb in range(CB):
+            nc.vector.tensor_tensor(window[cb][:].indirect(offsets[:]), sel_r[cb][:], mem_sb[cb][:], MULT)
             nc.sync.dma_start(out.rearrange("(p b) s -> p b s", b=CB)[:, cb, :], window[cb][:])

import concourse.masks as masks
import concourse.mybir as mybir

P = 128
C, K, S, N = 256, 256, 512, 128
CB, KB = C // P, K // P
FLOPS = 2 * C * K * N + 2 * K * C * N

BF16, F32, U16 = mybir.dt.bfloat16, mybir.dt.float32, mybir.dt.uint16
EXP, TANH = mybir.ActivationFunctionType.Exp, mybir.ActivationFunctionType.Tanh
MULT = mybir.AluOpType.mult
WARM_UP = 3


def tile_metaembedding_classifier_kernel(tc, base, x, w_hall, b_hall, centroids, b_sel, offs, out):
    nc = tc.nc
    with (
        tc.tile_pool(name="held", bufs=1) as held,
        tc.psum_pool(name="psum", bufs=1) as psum,
    ):
        x_sb = held.tile([P, CB, N], BF16, name="x_sb")
        nc.sync.dma_start(x_sb[:], x.rearrange("(p b) j -> p b j", b=CB))
        w_sb = held.tile([P, CB, K], BF16, name="w_sb")
        nc.sync.dma_start(w_sb[:], w_hall.rearrange("(p b) k -> p b k", b=CB))
        b_sel_sb = held.tile([P, CB], F32, name="b_sel_sb")
        nc.sync.dma_start(b_sel_sb[:], b_sel.rearrange("(p b) o -> p (b o)", b=CB))
        b_hall_sb = held.tile([P, KB], F32, name="b_hall_sb")
        nc.sync.dma_start(b_hall_sb[:], b_hall.rearrange("(p b) o -> p (b o)", b=KB))
        cent_sb = held.tile([P, KB, C], BF16, name="cent_sb")
        nc.sync.dma_start(cent_sb[:], centroids.rearrange("(p b) c -> p b c", b=KB))
        offsets = held.tile([P, N // 16], U16, name="offsets")
        nc.sync.dma_start(offsets[:], offs)
        window = [held.tile([P, S], F32, name=f"window{cb}") for cb in range(CB)]
        for cb in range(CB):
            nc.sync.dma_start(window[cb][:], base.rearrange("(p b) s -> p b s", b=CB)[:, cb, :])

        zeros = held.tile([P, P], BF16, name="zeros")
        nc.gpsimd.memset(zeros[:], 0.0)
        unused = psum.tile([P, 4, P], F32, name="unused")
        for i in range(WARM_UP):
            nc.tensor.matmul(unused[:], zeros[:], zeros[:].unsqueeze(1).to_broadcast([P, 4, P]), start=True, stop=True)
        ones = held.tile([P, 1], BF16, name="ones")
        nc.gpsimd.memset(ones[:], 1.0)
        identity = held.tile([P, P], F32, name="identity")
        masks.make_identity(nc, identity[:])

        early = held.tile([P, 1], F32, name="early")
        nc.scalar.activation(early[:], zeros[:, 0:1], EXP)

        sel = [held.tile([P, N], F32, name=f"sel{cb}") for cb in range(CB)]
        for cb in range(CB):
            nc.scalar.activation(sel[cb][:], x_sb[:, cb, :], TANH, bias=b_sel_sb[:, cb : cb + 1])

        e_sb = [held.tile([P, N], BF16, name=f"e_sb{kb}") for kb in range(KB)]
        for kb in range(KB):
            z = psum.tile([P, N], F32, name=f"z{kb}")
            for b in range(CB):
                nc.tensor.matmul(z[:], w_sb[:, b, kb::KB], x_sb[:, b, :], start=(b == 0), stop=(b == CB - 1))
            nc.scalar.activation(e_sb[kb][:], z[:], EXP, bias=b_hall_sb[:, kb : kb + 1])

        e_sum = psum.tile([P, 1], F32, name="e_sum")
        for kb in range(KB):
            nc.tensor.matmul(e_sum[:], e_sb[kb][:], ones[:, 0:1], start=(kb == 0), stop=(kb == KB - 1))
        r_sum = held.tile([P, 1], F32, name="r_sum")
        nc.vector.reciprocal(r_sum[:], e_sum[:])

        r_all = psum.tile([P, N], F32, name="r_all")
        nc.tensor.transpose(r_all[:], r_sum[:, 0:1].to_broadcast([P, P]), identity[:])

        mem_sb = [held.tile([P, N], F32, name=f"mem_sb{cb}") for cb in range(CB)]
        for cb in range(CB):
            mem = psum.tile([P, N], F32, name=f"mem{cb}")
            for kb in range(KB):
                nc.tensor.matmul(mem[:], cent_sb[:, kb, cb::CB], e_sb[kb][:], start=(kb == 0), stop=(kb == KB - 1))
            nc.vector.tensor_copy(mem_sb[cb][:], mem[:])

        sel_r = [held.tile([P, N], F32, name=f"sel_r{cb}") for cb in range(CB)]
        for cb in range(CB):
            nc.vector.tensor_tensor(sel_r[cb][:], sel[cb][:], r_all[:], MULT)
        for cb in range(CB):
            nc.vector.tensor_tensor(window[cb][:].indirect(offsets[:]), sel_r[cb][:], mem_sb[cb][:], MULT)
            nc.sync.dma_start(out.rearrange("(p b) s -> p b s", b=CB)[:, cb, :], window[cb][:])
